import numpy as np
import ml_dtypes


def mxq(x, axis, fmt="e4m3"):
    dtype, down = {"e4m3": (ml_dtypes.float8_e4m3fn, 7), "e5m2": (ml_dtypes.float8_e5m2, 14)}[fmt]
    v = np.moveaxis(np.asarray(x, np.float32).astype(ml_dtypes.bfloat16).astype(np.float64), axis, -1)
    blocks = v.reshape(v.shape[:-1] + (-1, 32))
    amax = np.abs(blocks).max(-1, keepdims=True)
    byte = np.maximum(np.where(amax > 0, np.frexp(amax)[1] - 1 + 127, 0) - down, 1)
    scale = np.exp2(byte - 127.0)
    codes = (blocks / scale).astype(np.float32).astype(dtype).astype(np.float64)
    return np.moveaxis((codes * scale).reshape(v.shape), -1, axis)


WIDE = False


def mx_kscale(k):
    if not WIDE:
        return np.ones(k)
    levels = np.array([10, -10, 5, -5, 0])
    a = np.random.permutation(np.resize(levels, k // 512 * 4)).reshape(k // 512, 4)
    idx = np.arange(k)
    return np.exp2(a[idx // 512, idx % 128 // 32])


BF16 = ml_dtypes.bfloat16


def bf(x):
    return np.asarray(x, np.float32).astype(BF16)


def f64(x):
    return np.asarray(x).astype(np.float64)


B, N_IN, N_HID, N_OUT = 1024, 512, 1024, 256


def setup_inputs():
    s = mx_kscale(N_HID)
    return {"x": bf(np.random.standard_normal((B, N_IN))),
            "s0": bf(np.tanh(0.8 * np.random.standard_normal((B, N_HID))) * s),
            "h1": bf(np.tanh(np.random.standard_normal((B, N_HID))) * s),
            "ug": bf(np.random.standard_normal((N_HID, N_IN)) * 0.7 / np.sqrt(N_IN)),
            "wg_w": bf(np.random.standard_normal((N_HID, N_HID)) * 1.2 / np.sqrt(N_HID) / s[None, :]),
            "wg_b": bf(np.random.standard_normal(N_HID) * 0.3),
            "uz": bf(np.random.standard_normal((N_HID, N_IN)) * 0.7 / np.sqrt(N_IN)),
            "wz_w": bf(np.random.standard_normal((N_HID, N_HID)) * 1.2 / np.sqrt(N_HID) / s[None, :]),
            "wz_b": bf(np.random.standard_normal(N_HID) * 0.3),
            "w4": bf(np.random.standard_normal((N_OUT, N_HID)) / np.sqrt(N_HID) / s[None, :])}


def reference(x, s0, h1, ug, wg_w, wg_b, uz, wz_w, wz_b, w4):
    xq = mxq(np.abs(f64(x)) + 0.1, 1, "e4m3")
    s = f64(s0)
    sq = mxq(s, 1, "e4m3")
    g = np.tanh((xq @ mxq(f64(ug), 1, "e4m3").T) + ((sq @ mxq(f64(wg_w), 1, "e4m3").T) + f64(wg_b)))
    z = np.tanh((xq @ mxq(f64(uz), 1, "e4m3").T) + ((sq @ mxq(f64(wz_w), 1, "e4m3").T) + f64(wz_b)))
    s1 = (1.0 - g) * f64(h1) + z * s
    return mxq(s1, 1, "e4m3") @ mxq(f64(w4), 1, "e4m3").T

@@ -1,0 +1,385 @@
+from contextlib import ExitStack
+
+import concourse.mybir as mybir
+from concourse.masks import make_identity
+
+FLOPS = 2 * 1024 * 1024 * 1536 * 2 + 2 * 1024 * 1024 * 256
+
+F32 = mybir.dt.float32
+BF16 = mybir.dt.bfloat16
+U32 = mybir.dt.uint32
+U8 = mybir.dt.uint8
+FP8X4 = mybir.dt.float8_e4m3fn_x4
+ACT = mybir.ActivationFunctionType
+ALU = mybir.AluOpType
+P = 128
+
+
+def tile_idrm_ann_pb_kernel(tc, x, s0, h1, ug, wg_w, wg_b, uz, wz_w, wz_b, w4, out):
+    nc = tc.nc
+    with ExitStack() as ctx:
+        keep = ctx.enter_context(tc.tile_pool(name="keep", bufs=1))
+        raww = ctx.enter_context(tc.tile_pool(name="raww", bufs=3))
+        grp = ctx.enter_context(tc.tile_pool(name="grp", bufs=3))
+        work = ctx.enter_context(tc.tile_pool(name="work", bufs=2))
+        psum = ctx.enter_context(tc.psum_pool(name="psum", bufs=8))
+        ctx.enter_context(tc.manual_schedule())
+
+        ident = keep.tile([P, P], F32, name="ident")
+        make_identity(nc, ident[:])
+        braw = keep.tile([P, P], F32, name="braw")
+        nc.vector.memset(braw[:], 0.0)
+        bias = keep.tile([P, 16], F32, name="bias")
+
+        x_sb = keep.tile([P, 8 * 512], BF16, name="x_sb")
+        s0_sb = keep.tile([P, 8 * 1024], BF16, name="s0_sb")
+        h1_sb = keep.tile([P, 8 * 1024], BF16, name="h1_sb")
+        w4_sb = keep.tile([P, 2 * 1024], BF16, name="w4_sb")
+        out_sb = keep.tile([P, 8 * 256], F32, name="out_sb")
+
+        s0G = [keep.tile([P, 4096], BF16, name="s0G%d" % c, align_bytes=64) for c in range(2)]
+        x_c = [keep.tile([P, 512], U32, name="x_c%d" % c, align_bytes=64) for c in range(2)]
+        x_s = [keep.tile([P, 512], U8, name="x_s%d" % c, align_bytes=64) for c in range(2)]
+        s0_c = [keep.tile([P, 1024], U32, name="s0_c%d" % c, align_bytes=64) for c in range(2)]
+        s0_s = [keep.tile([P, 1024], U8, name="s0_s%d" % c, align_bytes=64) for c in range(2)]
+        w_c = {}
+        w_s = {}
+        for G in range(4):
+            for gate in range(2):
+                w_c[(G, gate)] = keep.tile([P, 768], U32, name="w_c%d%d" % (G, gate), align_bytes=64)
+                w_s[(G, gate)] = keep.tile([P, 768], U8, name="w_s%d%d" % (G, gate), align_bytes=64)
+        w4_c = keep.tile([P, 512], U32, name="w4_c", align_bytes=64)
+        w4_s = keep.tile([P, 512], U8, name="w4_s", align_bytes=64)
+        s1_c = {}
+        s1_s = {}
+        for c in range(2):
+            for g in range(2):
+                s1_c[(c, g)] = keep.tile([P, 512], U32, name="s1_c%d%d" % (c, g), align_bytes=64)
+                s1_s[(c, g)] = keep.tile([P, 512], U8, name="s1_s%d%d" % (c, g), align_bytes=64)
+
+        def load_rows(dst, src, c, width):
+            cols = slice(c * 4 * width, (c + 1) * 4 * width)
+            nc.sync.dma_start(out=dst[:, cols], in_=src.rearrange("(p r) k -> p (r k)", r=8)[:, cols])
+
+        raw = {}
+
+        def load_w(G):
+            for nm, src, width in (("ug", ug, 512), ("wg", wg_w, 1024), ("uz", uz, 512), ("wz", wz_w, 1024)):
+                t = raww.tile([P, 2 * width], BF16, name="raw_%s%d" % (nm, G), tag="raw_" + nm)
+                nc.sync.dma_start(
+                    out=t[:], in_=src[256 * G : 256 * G + 256, :].rearrange("(j e) k -> j (e k)", e=2)
+                )
+                raw[(nm, G)] = t
+
+        bview = braw[:].bitcast(BF16)
+        nc.scalar.dma_start(out=bview[0:4, :], in_=wg_b.rearrange("(a w) -> a w", a=4))
+        nc.scalar.dma_start(out=bview[4:8, :], in_=wz_b.rearrange("(a w) -> a w", a=4))
+        load_rows(x_sb, x, 0, 512)
+        load_rows(s0_sb, s0, 0, 1024)
+        load_w(0)
+        load_w(1)
+        load_rows(h1_sb, h1, 0, 1024)
+        load_w(2)
+
+        def new_bank(nm):
+            return psum.tile([P, 512], F32, name=nm, tag="bank")
+
+        def transposes(nm, srcs):
+            bank = new_bank(nm)
+            for i, src in enumerate(srcs):
+                nc.tensor.transpose(bank[:, i * P : (i + 1) * P], src, ident[:])
+            return bank
+
+        def evac_words(eng, dst_words, bank):
+            o = dst_words.rearrange("p (n u) -> p n u", u=2)
+            i = bank[:].rearrange("p (u n) -> p n u", u=2)
+            if eng == "S":
+                nc.scalar.copy(out=o, in_=i)
+            else:
+                nc.vector.tensor_copy(out=o, in_=i)
+
+        def quant(codes, scales, src, a, b):
+            nc.vector.quantize_mx(out=codes[:, a:b].bitcast(FP8X4), scales=scales[:, a:b], in_=src[:, 4 * a : 4 * b])
+
+        xw = x_sb[:].bitcast(F32)
+        s0w = s0_sb[:].bitcast(F32)
+        h1w = h1_sb[:].bitcast(F32)
+        w4w = w4_sb[:].bitcast(F32)
+        xG = {}
+
+        def prep_x(c, h):
+            if h == 0:
+                xG[c] = grp.tile([P, 2048], BF16, name="xG%d" % c, tag="wG", align_bytes=64)
+            srcs = []
+            for u in range(2):
+                for rr in range(2):
+                    o = (4 * c + 2 * h + rr) * 256 + u * P
+                    srcs.append(xw[:, o : o + P])
+            bank = transposes("tx%d%d" % (c, h), srcs)
+            dst = xG[c][:, h * 1024 : (h + 1) * 1024]
+            nc.scalar.activation(
+                out=dst.rearrange("p (n u e) -> p n u e", u=2, e=2),
+                in_=bank[:].bitcast(BF16).rearrange("p (u n e) -> p n u e", u=2, e=2),
+                func=ACT.Abs,
+            )
+
+        def add_x(c, h):
+            dst = xG[c][:, h * 1024 : (h + 1) * 1024]
+            nc.vector.tensor_scalar_add(out=dst, in0=dst, scalar1=0.1)
+
+        def prep_s0(c, g, h, eng):
+            srcs = []
+            for u in range(2):
+                for rr in range(2):
+                    o = (4 * c + 2 * h + rr) * 512 + g * 256 + u * P
+                    srcs.append(s0w[:, o : o + P])
+            bank = transposes("ts%d%d%d" % (c, g, h), srcs)
+            o = (g * 512 + h * 256) * 2
+            evac_words(eng, s0G[c][:].bitcast(F32)[:, o : o + 512], bank)
+
+        wG = {}
+
+        def prep_w(G, gate, k, eng):
+            if k == 0:
+                wG[(G, gate)] = grp.tile([P, 3072], BF16, name="wG%d%d" % (G, gate), tag="wG", align_bytes=64)
+            srcs = []
+            for u in range(2):
+                for e in range(2):
+                    if k == 0:
+                        t = raw[(("ug", "uz")[gate], G)]
+                        o = e * 256 + u * P
+                    else:
+                        t = raw[(("wg", "wz")[gate], G)]
+                        o = e * 512 + (k - 1) * 256 + u * P
+                    srcs.append(t[:].bitcast(F32)[:, o : o + P])
+            bank = transposes("tw%d%d%d" % (G, gate, k), srcs)
+            evac_words(eng, wG[(G, gate)][:].bitcast(F32)[:, k * 512 : (k + 1) * 512], bank)
+
+        def quant_w(G, gate):
+            quant(w_c[(G, gate)], w_s[(G, gate)], wG[(G, gate)], 0, 512)
+            quant(w_c[(G, gate)], w_s[(G, gate)], wG[(G, gate)], 512, 768)
+
+        hp = {}
+
+        def prep_h1(G, c):
+            srcs = []
+            for rr in range(4):
+                o = (4 * c + rr) * 512 + G * P
+                srcs.append(h1w[:, o : o + P])
+            hp[(G, c)] = transposes("th%d%d" % (G, c), srcs)
+
+        GT = {}
+        ZT = {}
+
+        def mx_group(G, gate, e, c):
+            g = G // 2
+            if G % 2 == 0 and e == 0:
+                if gate == 0:
+                    GT[(g, c)] = work.tile([P, 2048], F32, name="GT%d%d" % (g, c), tag="GT")
+                else:
+                    ZT[(g, c)] = work.tile([P, 2048], F32, name="ZT%d%d" % (g, c), tag="ZT")
+            acc = new_bank("acc%d%d%d%d" % (G, gate, e, c))
+            wc = w_c[(G, gate)]
+            ws = w_s[(G, gate)]
+            for k in range(3):
+                if k == 0:
+                    rc, rs, o = x_c[c], x_s[c], 0
+                else:
+                    rc, rs, o = s0_c[c], s0_s[c], (k - 1) * 512
+                a = k * 256 + e * P
+                nc.tensor.matmul_mx(
+                    out=acc[:],
+                    lhsT=wc[:, a : a + P].bitcast(FP8X4),
+                    lhsT_scale=ws[:, a : a + P],
+                    rhs=rc[:, o : o + 512].bitcast(FP8X4),
+                    rhs_scale=rs[:, o : o + 512],
+                    start=(k == 0),
+                    stop=(k == 2),
+                )
+            t = 2 * (G % 2) + e
+            dst = (GT, ZT)[gate][(g, c)][:, t * 512 : (t + 1) * 512]
+            col = (gate * 4 + G) * 2 + e
+            nc.scalar.activation(out=dst, in_=acc[:], func=ACT.Tanh, bias=bias[:, col : col + 1], scale=1.0)
+
+        def p1(G, e, c):
+            t = 2 * (G % 2) + e
+            d = GT[(G // 2, c)][:, t * 512 : (t + 1) * 512]
+            hv = hp[(G, c)][:].bitcast(BF16).rearrange("p (n e) -> p n e", e=2)[:, :, e]
+            nc.vector.scalar_tensor_tensor(out=d, in0=d, scalar=-1.0, in1=hv, op0=ALU.add, op1=ALU.mult)
+
+        def p2(G, e, c):
+            g = G // 2
+            t = 2 * (G % 2) + e
+            d = ZT[(g, c)][:, t * 512 : (t + 1) * 512]
+            sv = s0G[c][:].rearrange("p (g n t) -> p g n t", g=2, t=4)[:, g, :, t]
+            nc.vector.tensor_tensor(out=d, in0=d, in1=sv, op=ALU.mult)
+
+        s1G = {}
+
+        def add_piece(g, c, q):
+            if q == 0:
+                s1G[(g, c)] = work.tile([P, 2048], BF16, name="s1G%d%d" % (g, c), tag="s1G", align_bytes=64)
+            n0 = q * P
+            o = s1G[(g, c)][:, 4 * n0 : 4 * (n0 + P)].rearrange("p (c i t) -> p c t i", i=4, t=4)
+            a = ZT[(g, c)][:].rearrange("p (t n) -> p t n", t=4)[:, :, n0 : n0 + P].rearrange("p t (c i) -> p c t i", i=4)
+            b = GT[(g, c)][:].rearrange("p (t n) -> p t n", t=4)[:, :, n0 : n0 + P].rearrange("p t (c i) -> p c t i", i=4)
+            nc.vector.tensor_tensor(out=o, in0=a, in1=b, op=ALU.subtract)
+
+        def stage2(c, h, eng):
+            bank = new_bank("o%d%d" % (c, h))
+            for rr in range(2):
+                a = (2 * h + rr) * P
+                for g in range(2):
+                    nc.tensor.matmul_mx(
+                        out=bank[:, rr * 256 : (rr + 1) * 256],
+                        lhsT=s1_c[(c, g)][:, a : a + P].bitcast(FP8X4),
+                        lhsT_scale=s1_s[(c, g)][:, a : a + P],
+                        rhs=w4_c[:, g * 256 : (g + 1) * 256].bitcast(FP8X4),
+                        rhs_scale=w4_s[:, g * 256 : (g + 1) * 256],
+                        start=(g == 0),
+                        stop=(g == 1),
+                    )
+            o = (4 * c + 2 * h) * 256
+            if eng == "S":
+                nc.scalar.copy(out=out_sb[:, o : o + 512], in_=bank[:])
+            else:
+                nc.vector.tensor_copy(out=out_sb[:, o : o + 512], in_=bank[:])
+
+        out_v = out.rearrange("(p r) n -> p (r n)", r=8)
+
+        def store(a, b):
+            nc.sync.dma_start(out=out_v[:, a:b], in_=out_sb[:, a:b])
+
+        fillers = []
+        done = [0]
+
+        def fill(n=1):
+            for i in range(n):
+                if done[0] < len(fillers):
+                    fillers[done[0]]()
+                    done[0] += 1
+
+        def queue_add(g, c):
+            for q in range(4):
+                fillers.append(lambda q=q: add_piece(g, c, q))
+            fillers.append(lambda: quant(s1_c[(c, g)], s1_s[(c, g)], s1G[(g, c)], 0, 512))
+
+        prep_x(0, 0)
+        prep_x(0, 1)
+        add_x(0, 0)
+        add_x(0, 1)
+        bbank = new_bank("bbank")
+        nc.tensor.transpose(bbank[:, 0:P], braw[:], ident[:])
+        nc.vector.tensor_copy(out=bias[:], in_=bbank[:].bitcast(BF16)[:, 0:16])
+        prep_s0(0, 0, 0, "V")
+        prep_s0(0, 0, 1, "S")
+        quant(x_c[0], x_s[0], xG[0], 0, 512)
+        prep_s0(0, 1, 0, "V")
+        prep_s0(0, 1, 1, "S")
+        quant(s0_c[0], s0_s[0], s0G[0], 0, 512)
+        prep_w(0, 0, 0, "V")
+        prep_w(0, 0, 1, "S")
+        quant(s0_c[0], s0_s[0], s0G[0], 512, 1024)
+        prep_w(0, 0, 2, "V")
+        prep_w(0, 1, 0, "S")
+        quant_w(0, 0)
+        prep_w(0, 1, 1, "V")
+        prep_w(0, 1, 2, "S")
+        prep_h1(0, 0)
+        quant_w(0, 1)
+        load_w(3)
+        load_rows(x_sb, x, 1, 512)
+        load_rows(s0_sb, s0, 1, 1024)
+        load_rows(h1_sb, h1, 1, 1024)
+        nc.sync.dma_start(out=w4_sb[:].rearrange("j (r k) -> j r k", r=2), in_=w4.rearrange("(r j) k -> j r k", j=P))
+
+        for G in range(4):
+            mx_group(G, 0, 0, 0)
+            mx_group(G, 0, 1, 0)
+            if G < 3:
+                for k in range(3):
+                    prep_w(G + 1, 0, k, "S")
+            else:
+                prep_x(1, 0)
+                prep_x(1, 1)
+                prep_s0(1, 0, 0, "S")
+            p1(G, 0, 0)
+            p1(G, 1, 0)
+            fill()
+            if G < 3:
+                quant_w(G + 1, 0)
+            else:
+                add_x(1, 0)
+                add_x(1, 1)
+            mx_group(G, 1, 0, 0)
+            mx_group(G, 1, 1, 0)
+            if G < 3:
+                for k in range(3):
+                    prep_w(G + 1, 1, k, "S")
+                prep_h1(G + 1, 0)
+            else:
+                prep_s0(1, 0, 1, "S")
+                prep_s0(1, 1, 0, "S")
+                prep_s0(1, 1, 1, "S")
+                prep_h1(0, 1)
+            p2(G, 0, 0)
+            p2(G, 1, 0)
+            if G < 3:
+                fill()
+                quant_w(G + 1, 1)
+            else:
+                quant(x_c[1], x_s[1], xG[1], 0, 512)
+                quant(s0_c[1], s0_s[1], s0G[1], 0, 512)
+                quant(s0_c[1], s0_s[1], s0G[1], 512, 1024)
+            if G % 2 == 1:
+                queue_add(G // 2, 0)
+            fill()
+
+        w4G = None
+        for G in range(4):
+            for gate in range(2):
+                for e in range(2):
+                    mx_group(G, gate, e, 1)
+            if G == 1:
+                stage2(0, 0, "S")
+                stage2(0, 1, "S")
+                store(0, 1024)
+            if G < 3:
+                prep_h1(G + 1, 1)
+            if G == 0:
+                w4G = grp.tile([P, 2048], BF16, name="w4G", tag="wG", align_bytes=64)
+                for g in range(2):
+                    srcs = []
+                    for u in range(2):
+                        for ro in range(2):
+                            o = ro * 512 + g * 256 + u * P
+                            srcs.append(w4w[:, o : o + P])
+                    bank = transposes("t4%d" % g, srcs)
+                    evac_words("S", w4G[:].bitcast(F32)[:, g * 512 : (g + 1) * 512], bank)
+            p1(G, 0, 1)
+            p1(G, 1, 1)
+            fill(2)
+            p2(G, 0, 1)
+            p2(G, 1, 1)
+            if G == 0:
+                fill(2)
+                quant(w4_c, w4_s, w4G, 0, 512)
+            if G == 1:
+                queue_add(0, 1)
+            if G < 3:
+                fill(1)
+
+        fill(8)
+        g, c = 1, 1
+        add_piece(g, c, 0)
+        add_piece(g, c, 1)
+        quant(s1_c[(c, g)], s1_s[(c, g)], s1G[(g, c)], 0, P)
+        add_piece(g, c, 2)
+        quant(s1_c[(c, g)], s1_s[(c, g)], s1G[(g, c)], P, 2 * P)
+        stage2(1, 0, "S")
+        store(1024, 1536)
+        add_piece(g, c, 3)
+        quant(s1_c[(c, g)], s1_s[(c, g)], s1G[(g, c)], 2 * P, 3 * P)
+        quant(s1_c[(c, g)], s1_s[(c, g)], s1G[(g, c)], 3 * P, 4 * P)
+        stage2(1, 1, "V")
+        store(1536, 2048)

@@ -31,9 +31,12 @@ def tile_idrm_ann_pb_kernel(tc, x, s0, h1, ug, wg_w, wg_b, uz, wz_w, wz_b, w4, o
         nc.vector.memset(braw[:], 0.0)
         bias = keep.tile([P, 16], F32, name="bias")
 
-        x_sb = keep.tile([P, 8 * 512], BF16, name="x_sb")
-        s0_sb = keep.tile([P, 8 * 1024], BF16, name="s0_sb")
-        h1_sb = keep.tile([P, 8 * 1024], BF16, name="h1_sb")
+        x_sb = [work.tile([P, 4 * 512], BF16, name="x_sb%d" % c, tag="xraw") for c in range(2)]
+        s0_sb = [work.tile([P, 4 * 1024], BF16, name="s0_sb%d" % c, tag="s0raw") for c in range(2)]
+        h1_sb = {}
+        for c in range(2):
+            for g in range(2):
+                h1_sb[(c, g)] = keep.tile([P, 4 * 512], BF16, name="h1_sb%d%d" % (c, g))
         w4_sb = keep.tile([P, 2 * 1024], BF16, name="w4_sb")
         out_sb = keep.tile([P, 8 * 256], F32, name="out_sb")
 
@@ -57,14 +60,16 @@ def tile_idrm_ann_pb_kernel(tc, x, s0, h1, ug, wg_w, wg_b, uz, wz_w, wz_b, w4, o
                 s1_c[(c, g)] = keep.tile([P, 512], U32, name="s1_c%d%d" % (c, g), align_bytes=64)
                 s1_s[(c, g)] = keep.tile([P, 512], U8, name="s1_s%d%d" % (c, g), align_bytes=64)
 
-        def load_rows(dst, src, c, width):
-            cols = slice(c * 4 * width, (c + 1) * 4 * width)
-            nc.sync.dma_start(out=dst[:, cols], in_=src.rearrange("(p r) k -> p (r k)", r=8)[:, cols])
+        def load_rows(dst, src, c, width, r0=0, r1=4):
+            nc.sync.dma_start(
+                out=dst[c][:, r0 * width : r1 * width],
+                in_=src.rearrange("(p r) k -> p (r k)", r=8)[:, (4 * c + r0) * width : (4 * c + r1) * width],
+            )
 
         raw = {}
 
-        def load_w(G):
-            for nm, src, width in (("ug", ug, 512), ("wg", wg_w, 1024), ("uz", uz, 512), ("wz", wz_w, 1024)):
+        def load_w(G, gate):
+            for nm, src, width in ((("ug", ug, 512), ("wg", wg_w, 1024)), (("uz", uz, 512), ("wz", wz_w, 1024)))[gate]:
                 t = raww.tile([P, 2 * width], BF16, name="raw_%s%d" % (nm, G), tag="raw_" + nm)
                 nc.sync.dma_start(
                     out=t[:], in_=src[256 * G : 256 * G + 256, :].rearrange("(j e) k -> j (e k)", e=2)
@@ -74,12 +79,24 @@ def tile_idrm_ann_pb_kernel(tc, x, s0, h1, ug, wg_w, wg_b, uz, wz_w, wz_b, w4, o
         bview = braw[:].bitcast(BF16)
         nc.scalar.dma_start(out=bview[0:4, :], in_=wg_b.rearrange("(a w) -> a w", a=4))
         nc.scalar.dma_start(out=bview[4:8, :], in_=wz_b.rearrange("(a w) -> a w", a=4))
+        def load_h1(c, g):
+            dv = h1_sb[(c, g)][:].rearrange("p (r k) -> p r k", r=4)
+            sv = h1.rearrange("(p r) k -> p r k", r=8)[:, 4 * c : 4 * c + 4, g * 512 : (g + 1) * 512]
+            nc.sync.dma_start(out=dv, in_=sv)
+
         load_rows(x_sb, x, 0, 512)
-        load_rows(s0_sb, s0, 0, 1024)
-        load_w(0)
-        load_w(1)
-        load_rows(h1_sb, h1, 0, 1024)
-        load_w(2)
+        load_w(0, 0)
+        load_rows(s0_sb, s0, 0, 1024, 0, 2)
+        load_rows(s0_sb, s0, 0, 1024, 2, 4)
+        load_w(0, 1)
+        load_w(1, 0)
+        load_h1(0, 0)
+        load_w(1, 1)
+        load_rows(x_sb, x, 1, 512)
+        load_rows(s0_sb, s0, 1, 1024)
+        load_h1(1, 0)
+        load_w(2, 0)
+        load_w(2, 1)
 
         def new_bank(nm):
             return psum.tile([P, 512], F32, name=nm, tag="bank")
@@ -101,9 +118,6 @@ def tile_idrm_ann_pb_kernel(tc, x, s0, h1, ug, wg_w, wg_b, uz, wz_w, wz_b, w4, o
         def quant(codes, scales, src, a, b):
             nc.vector.quantize_mx(out=codes[:, a:b].bitcast(FP8X4), scales=scales[:, a:b], in_=src[:, 4 * a : 4 * b])
 
-        xw = x_sb[:].bitcast(F32)
-        s0w = s0_sb[:].bitcast(F32)
-        h1w = h1_sb[:].bitcast(F32)
         w4w = w4_sb[:].bitcast(F32)
         xG = {}
 
@@ -113,8 +127,8 @@ def tile_idrm_ann_pb_kernel(tc, x, s0, h1, ug, wg_w, wg_b, uz, wz_w, wz_b, w4, o
             srcs = []
             for u in range(2):
                 for rr in range(2):
-                    o = (4 * c + 2 * h + rr) * 256 + u * P
-                    srcs.append(xw[:, o : o + P])
+                    o = (2 * h + rr) * 256 + u * P
+                    srcs.append(x_sb[c][:].bitcast(F32)[:, o : o + P])
             bank = transposes("tx%d%d" % (c, h), srcs)
             dst = xG[c][:, h * 1024 : (h + 1) * 1024]
             nc.scalar.activation(
@@ -131,8 +145,8 @@ def tile_idrm_ann_pb_kernel(tc, x, s0, h1, ug, wg_w, wg_b, uz, wz_w, wz_b, w4, o
             srcs = []
             for u in range(2):
                 for rr in range(2):
-                    o = (4 * c + 2 * h + rr) * 512 + g * 256 + u * P
-                    srcs.append(s0w[:, o : o + P])
+                    o = (2 * h + rr) * 512 + g * 256 + u * P
+                    srcs.append(s0_sb[c][:].bitcast(F32)[:, o : o + P])
             bank = transposes("ts%d%d%d" % (c, g, h), srcs)
             o = (g * 512 + h * 256) * 2
             evac_words(eng, s0G[c][:].bitcast(F32)[:, o : o + 512], bank)
@@ -164,65 +178,70 @@ def tile_idrm_ann_pb_kernel(tc, x, s0, h1, ug, wg_w, wg_b, uz, wz_w, wz_b, w4, o
         def prep_h1(G, c):
             srcs = []
             for rr in range(4):
-                o = (4 * c + rr) * 512 + G * P
-                srcs.append(h1w[:, o : o + P])
+                o = rr * 256 + (G % 2) * P
+                srcs.append(h1_sb[(c, G // 2)][:].bitcast(F32)[:, o : o + P])
             hp[(G, c)] = transposes("th%d%d" % (G, c), srcs)
 
         GT = {}
         ZT = {}
 
-        def mx_group(G, gate, e, c):
+        def mx_group(G, gate, e, c, n0=0, N=512):
             g = G // 2
             if G % 2 == 0 and e == 0:
                 if gate == 0:
-                    GT[(g, c)] = work.tile([P, 2048], F32, name="GT%d%d" % (g, c), tag="GT")
+                    GT[(g, c, n0)] = work.tile(
+                        [P, 4 * N], F32, name="GT%d%d%d" % (g, c, n0), tag=("GT" if N == 512 else "xraw")
+                    )
                 else:
-                    ZT[(g, c)] = work.tile([P, 2048], F32, name="ZT%d%d" % (g, c), tag="ZT")
-            acc = new_bank("acc%d%d%d%d" % (G, gate, e, c))
+                    ZT[(g, c, n0)] = work.tile(
+                        [P, 4 * N], F32, name="ZT%d%d%d" % (g, c, n0), tag=("ZT" if N == 512 else "s0raw")
+                    )
+            acc = new_bank("acc%d%d%d%d%d" % (G, gate, e, c, n0))
             wc = w_c[(G, gate)]
             ws = w_s[(G, gate)]
             for k in range(3):
                 if k == 0:
-                    rc, rs, o = x_c[c], x_s[c], 0
+                    rc, rs, o = x_c[c], x_s[c], n0
                 else:
-                    rc, rs, o = s0_c[c], s0_s[c], (k - 1) * 512
+                    rc, rs, o = s0_c[c], s0_s[c], (k - 1) * 512 + n0
                 a = k * 256 + e * P
                 nc.tensor.matmul_mx(
-                    out=acc[:],
+                    out=acc[:, 0:N],
                     lhsT=wc[:, a : a + P].bitcast(FP8X4),
                     lhsT_scale=ws[:, a : a + P],
-                    rhs=rc[:, o : o + 512].bitcast(FP8X4),
-                    rhs_scale=rs[:, o : o + 512],
+                    rhs=rc[:, o : o + N].bitcast(FP8X4),
+                    rhs_scale=rs[:, o : o + N],
                     start=(k == 0),
                     stop=(k == 2),
                 )
             t = 2 * (G % 2) + e
-            dst = (GT, ZT)[gate][(g, c)][:, t * 512 : (t + 1) * 512]
+            dst = (GT, ZT)[gate][(g, c, n0)][:, t * N : (t + 1) * N]
             col = (gate * 4 + G) * 2 + e
-            nc.scalar.activation(out=dst, in_=acc[:], func=ACT.Tanh, bias=bias[:, col : col + 1], scale=1.0)
+            nc.scalar.activation(out=dst, in_=acc[:, 0:N], func=ACT.Tanh, bias=bias[:, col : col + 1], scale=1.0)
 
-        def p1(G, e, c):
-            t = 2 * (G % 2) + e
-            d = GT[(G // 2, c)][:, t * 512 : (t + 1) * 512]
-            hv = hp[(G, c)][:].bitcast(BF16).rearrange("p (n e) -> p n e", e=2)[:, :, e]
+        def p1(G, c, n0=0, N=512):
+            u = G % 2
+            d = GT[(G // 2, c, n0)][:, 2 * u * N : (2 * u + 2) * N].rearrange("p (t n) -> p t n", t=2)
+            hv = hp[(G, c)][:].bitcast(BF16).rearrange("p (n e) -> p e n", e=2)[:, :, n0 : n0 + N]
             nc.vector.scalar_tensor_tensor(out=d, in0=d, scalar=-1.0, in1=hv, op0=ALU.add, op1=ALU.mult)
 
-        def p2(G, e, c):
+        def p2(G, c, n0=0, N=512):
             g = G // 2
-            t = 2 * (G % 2) + e
-            d = ZT[(g, c)][:, t * 512 : (t + 1) * 512]
-            sv = s0G[c][:].rearrange("p (g n t) -> p g n t", g=2, t=4)[:, g, :, t]
+            u = G % 2
+            d = ZT[(g, c, n0)][:, 2 * u * N : (2 * u + 2) * N].rearrange("p (t n) -> p t n", t=2)
+            sv = s0G[c][:].rearrange("p (g n t) -> p g t n", g=2, t=4)[:, g, 2 * u : 2 * u + 2, n0 : n0 + N]
             nc.vector.tensor_tensor(out=d, in0=d, in1=sv, op=ALU.mult)
 
         s1G = {}
 
-        def add_piece(g, c, q):
+        def add_piece(g, c, q, n0=0):
             if q == 0:
                 s1G[(g, c)] = work.tile([P, 2048], BF16, name="s1G%d%d" % (g, c), tag="s1G", align_bytes=64)
-            n0 = q * P
-            o = s1G[(g, c)][:, 4 * n0 : 4 * (n0 + P)].rearrange("p (c i t) -> p c t i", i=4, t=4)
-            a = ZT[(g, c)][:].rearrange("p (t n) -> p t n", t=4)[:, :, n0 : n0 + P].rearrange("p t (c i) -> p c t i", i=4)
-            b = GT[(g, c)][:].rearrange("p (t n) -> p t n", t=4)[:, :, n0 : n0 + P].rearrange("p t (c i) -> p c t i", i=4)
+            m0 = q * P
+            o = s1G[(g, c)][:, 4 * m0 : 4 * (m0 + P)].rearrange("p (c i t) -> p c t i", i=4, t=4)
+            lo = m0 - n0
+            a = ZT[(g, c, n0)][:].rearrange("p (t n) -> p t n", t=4)[:, :, lo : lo + P].rearrange("p t (c i) -> p c t i", i=4)
+            b = GT[(g, c, n0)][:].rearrange("p (t n) -> p t n", t=4)[:, :, lo : lo + P].rearrange("p t (c i) -> p c t i", i=4)
             nc.vector.tensor_tensor(out=o, in0=a, in1=b, op=ALU.subtract)
 
         def stage2(c, h, eng):
@@ -245,6 +264,38 @@ def tile_idrm_ann_pb_kernel(tc, x, s0, h1, ug, wg_w, wg_b, uz, wz_w, wz_b, w4, o
             else:
                 nc.vector.tensor_copy(out=out_sb[:, o : o + 512], in_=bank[:])
 
+        obank = {}
+
+        def stage2_open(c, rr):
+            obank[(c, rr)] = new_bank("oo%d%d" % (c, rr))
+            a = rr * P
+            nc.tensor.matmul_mx(
+                out=obank[(c, rr)][:, 0:256],
+                lhsT=s1_c[(c, 0)][:, a : a + P].bitcast(FP8X4),
+                lhsT_scale=s1_s[(c, 0)][:, a : a + P],
+                rhs=w4_c[:, 0:256].bitcast(FP8X4),
+                rhs_scale=w4_s[:, 0:256],
+                start=True,
+                stop=False,
+            )
+
+        def stage2_close(c, rr, eng):
+            a = rr * P
+            nc.tensor.matmul_mx(
+                out=obank[(c, rr)][:, 0:256],
+                lhsT=s1_c[(c, 1)][:, a : a + P].bitcast(FP8X4),
+                lhsT_scale=s1_s[(c, 1)][:, a : a + P],
+                rhs=w4_c[:, 256:512].bitcast(FP8X4),
+                rhs_scale=w4_s[:, 256:512],
+                start=False,
+                stop=True,
+            )
+            o = (4 * c + rr) * 256
+            if eng == "S":
+                nc.scalar.copy(out=out_sb[:, o : o + 256], in_=obank[(c, rr)][:, 0:256])
+            else:
+                nc.vector.tensor_copy(out=out_sb[:, o : o + 256], in_=obank[(c, rr)][:, 0:256])
+
         out_v = out.rearrange("(p r) n -> p (r n)", r=8)
 
         def store(a, b):
@@ -264,122 +315,169 @@ def tile_idrm_ann_pb_kernel(tc, x, s0, h1, ug, wg_w, wg_b, uz, wz_w, wz_b, w4, o
                 fillers.append(lambda q=q: add_piece(g, c, q))
             fillers.append(lambda: quant(s1_c[(c, g)], s1_s[(c, g)], s1G[(g, c)], 0, 512))
 
+        def qs0h(c, g, h):
+            quant(s0_c[c], s0_s[c], s0G[c], g * 512 + h * 256, g * 512 + (h + 1) * 256)
+
         prep_x(0, 0)
         prep_x(0, 1)
+        prep_w(0, 0, 0, "V")
         add_x(0, 0)
+        prep_w(0, 0, 1, "V")
+        prep_w(0, 0, 2, "V")
         add_x(0, 1)
         bbank = new_bank("bbank")
         nc.tensor.transpose(bbank[:, 0:P], braw[:], ident[:])
-        nc.vector.tensor_copy(out=bias[:], in_=bbank[:].bitcast(BF16)[:, 0:16])
-        prep_s0(0, 0, 0, "V")
-        prep_s0(0, 0, 1, "S")
-        quant(x_c[0], x_s[0], xG[0], 0, 512)
-        prep_s0(0, 1, 0, "V")
-        prep_s0(0, 1, 1, "S")
-        quant(s0_c[0], s0_s[0], s0G[0], 0, 512)
-        prep_w(0, 0, 0, "V")
-        prep_w(0, 0, 1, "S")
-        quant(s0_c[0], s0_s[0], s0G[0], 512, 1024)
-        prep_w(0, 0, 2, "V")
-        prep_w(0, 1, 0, "S")
         quant_w(0, 0)
-        prep_w(0, 1, 1, "V")
-        prep_w(0, 1, 2, "S")
-        prep_h1(0, 0)
+        prep_s0(0, 0, 0, "S")
+        prep_s0(0, 1, 0, "S")
+        quant(x_c[0], x_s[0], xG[0], 0, 512)
+        nc.vector.tensor_copy(out=bias[:], in_=bbank[:].bitcast(BF16)[:, 0:16])
+        qs0h(0, 0, 0)
+        prep_s0(0, 0, 1, "S")
+        prep_s0(0, 1, 1, "V")
+        qs0h(0, 1, 0)
+        qs0h(0, 0, 1)
+        qs0h(0, 1, 1)
+        prep_w(0, 1, 0, "S")
+        prep_w(0, 1, 1, "S")
+        prep_w(0, 1, 2, "V")
         quant_w(0, 1)
-        load_w(3)
-        load_rows(x_sb, x, 1, 512)
-        load_rows(s0_sb, s0, 1, 1024)
-        load_rows(h1_sb, h1, 1, 1024)
+        load_w(3, 0)
+        load_w(3, 1)
+        load_h1(0, 1)
+        load_h1(1, 1)
         nc.sync.dma_start(out=w4_sb[:].rearrange("j (r k) -> j r k", r=2), in_=w4.rearrange("(r j) k -> j r k", j=P))
 
-        for G in range(4):
-            mx_group(G, 0, 0, 0)
-            mx_group(G, 0, 1, 0)
-            if G < 3:
-                for k in range(3):
-                    prep_w(G + 1, 0, k, "S")
+        def prep_w4():
+            w4G = grp.tile([P, 2048], BF16, name="w4G", tag="wG", align_bytes=64)
+            for g in range(2):
+                srcs = []
+                for u in range(2):
+                    for ro in range(2):
+                        o = ro * 512 + g * 256 + u * P
+                        srcs.append(w4w[:, o : o + P])
+                bank = transposes("t4%d" % g, srcs)
+                evac_words("S", w4G[:].bitcast(F32)[:, g * 512 : (g + 1) * 512], bank)
+            return w4G
+
+        def w3(G, gate, engs="SSS"):
+            for k in range(3):
+                prep_w(G, gate, k, engs[k])
+
+        hold = {}
+
+        def qw(G, gate, part):
+            if part == 0:
+                quant(w_c[(G, gate)], w_s[(G, gate)], wG[(G, gate)], 0, 512)
             else:
+                quant(w_c[(G, gate)], w_s[(G, gate)], wG[(G, gate)], 512, 768)
+
+        def qs0(c, g):
+            quant(s0_c[c], s0_s[c], s0G[c], g * 512, (g + 1) * 512)
+
+        def slot(r):
+            if r == 0:
+                prep_h1(0, 0)
+                w3(1, 0, "SVS")
+            elif r == 1:
+                w3(1, 1, "SVS")
                 prep_x(1, 0)
                 prep_x(1, 1)
+            elif r == 2:
+                prep_h1(1, 0)
                 prep_s0(1, 0, 0, "S")
-            p1(G, 0, 0)
-            p1(G, 1, 0)
-            fill()
-            if G < 3:
-                quant_w(G + 1, 0)
-            else:
+                prep_s0(1, 0, 1, "S")
+                prep_s0(1, 1, 0, "V")
+                prep_s0(1, 1, 1, "S")
+            elif r == 3:
+                prep_h1(0, 1)
+                w3(2, 0)
+            elif r == 5:
+                prep_h1(1, 1)
+                w3(2, 1)
+                prep_w(3, 0, 0, "S")
+            elif r == 7:
+                prep_h1(2, 0)
+                prep_w(3, 0, 1, "S")
+                prep_w(3, 0, 2, "S")
+                prep_w(3, 1, 0, "S")
+                prep_w(3, 1, 1, "S")
+            elif r == 9:
+                prep_h1(3, 0)
+                prep_w(3, 1, 2, "S")
+            elif r == 11:
+                prep_h1(2, 1)
+                prep_h1(3, 1)
+                hold["w4G"] = prep_w4()
+
+        def vitems(r):
+            if r == 0:
+                quant_w(1, 0)
+            elif r == 1:
+                quant_w(1, 1)
                 add_x(1, 0)
                 add_x(1, 1)
-            mx_group(G, 1, 0, 0)
-            mx_group(G, 1, 1, 0)
-            if G < 3:
-                for k in range(3):
-                    prep_w(G + 1, 1, k, "S")
-                prep_h1(G + 1, 0)
-            else:
-                prep_s0(1, 0, 1, "S")
-                prep_s0(1, 1, 0, "S")
-                prep_s0(1, 1, 1, "S")
-                prep_h1(0, 1)
-            p2(G, 0, 0)
-            p2(G, 1, 0)
-            if G < 3:
-                fill()
-                quant_w(G + 1, 1)
-            else:
+            elif r == 2:
                 quant(x_c[1], x_s[1], xG[1], 0, 512)
-                quant(s0_c[1], s0_s[1], s0G[1], 0, 512)
-                quant(s0_c[1], s0_s[1], s0G[1], 512, 1024)
-            if G % 2 == 1:
-                queue_add(G // 2, 0)
-            fill()
+                qs0(1, 0)
+                qs0(1, 1)
+            elif r == 3:
+                quant_w(2, 0)
+            elif r == 5:
+                quant_w(2, 1)
+            elif r == 7:
+                quant_w(3, 0)
+                qw(3, 1, 0)
+            elif r == 9:
+                qw(3, 1, 1)
+            elif r == 11:
+                quant(w4_c, w4_s, hold["w4G"], 0, 512)
 
-        w4G = None
-        for G in range(4):
+        order = ((0, 0), (1, 0), (0, 1), (1, 1), (2, 0), (3, 0))
+        for pi, (G, c) in enumerate(order):
             for gate in range(2):
-                for e in range(2):
-                    mx_group(G, gate, e, 1)
-            if G == 1:
-                stage2(0, 0, "S")
-                stage2(0, 1, "S")
-                store(0, 1024)
-            if G < 3:
-                prep_h1(G + 1, 1)
-            if G == 0:
-                w4G = grp.tile([P, 2048], BF16, name="w4G", tag="wG", align_bytes=64)
-                for g in range(2):
-                    srcs = []
-                    for u in range(2):
-                        for ro in range(2):
-                            o = ro * 512 + g * 256 + u * P
-                            srcs.append(w4w[:, o : o + P])
-                    bank = transposes("t4%d" % g, srcs)
-                    evac_words("S", w4G[:].bitcast(F32)[:, g * 512 : (g + 1) * 512], bank)
-            p1(G, 0, 1)
-            p1(G, 1, 1)
-            fill(2)
-            p2(G, 0, 1)
-            p2(G, 1, 1)
-            if G == 0:
-                fill(2)
-                quant(w4_c, w4_s, w4G, 0, 512)
-            if G == 1:
-                queue_add(0, 1)
-            if G < 3:
-                fill(1)
+                r = 2 * pi + gate
+                mx_group(G, gate, 0, c)
+                mx_group(G, gate, 1, c)
+                slot(r)
+                if r == 9:
+                    vitems(r)
+                if gate == 0:
+                    p1(G, c)
+                else:
+                    p2(G, c)
+                fill()
+                if r != 9:
+                    vitems(r)
+                if gate == 1 and G % 2 == 1:
+                    queue_add(G // 2, c)
+                fill()
 
-        fill(8)
         g, c = 1, 1
-        add_piece(g, c, 0)
-        add_piece(g, c, 1)
-        quant(s1_c[(c, g)], s1_s[(c, g)], s1G[(g, c)], 0, P)
-        add_piece(g, c, 2)
-        quant(s1_c[(c, g)], s1_s[(c, g)], s1G[(g, c)], P, 2 * P)
-        stage2(1, 0, "S")
+        for hh in range(2):
+            n0 = hh * 256
+            for G in (2, 3):
+                for gate in range(2):
+                    for e in range(2):
+                        mx_group(G, gate, e, 1, n0, 256)
+                p1(G, 1, n0, 256)
+                fill(1)
+                p2(G, 1, n0, 256)
+                fill(1)
+            fill(8)
+            add_piece(g, c, 2 * hh, n0)
+            add_piece(g, c, 2 * hh + 1, n0)
+            quant(s1_c[(c, g)], s1_s[(c, g)], s1G[(g, c)], 2 * hh * P, (2 * hh + 1) * P)
+            quant(s1_c[(c, g)], s1_s[(c, g)], s1G[(g, c)], (2 * hh + 1) * P, (2 * hh + 2) * P)
+        stage2(0, 0, "S")
+        stage2(0, 1, "S")
+        store(0, 1024)
+        for rr in range(4):
+            stage2_open(1, rr)
+        stage2_close(1, 0, "S")
+        stage2_close(1, 1, "S")
         store(1024, 1536)
-        add_piece(g, c, 3)
-        quant(s1_c[(c, g)], s1_s[(c, g)], s1G[(g, c)], 2 * P, 3 * P)
-        quant(s1_c[(c, g)], s1_s[(c, g)], s1G[(g, c)], 3 * P, 4 * P)
-        stage2(1, 1, "V")
-        store(1536, 2048)
+        stage2_close(1, 2, "S")
+        store(1536, 1792)
+        stage2_close(1, 3, "V")
+        store(1792, 2048)

@@ -85,18 +85,18 @@ def tile_idrm_ann_pb_kernel(tc, x, s0, h1, ug, wg_w, wg_b, uz, wz_w, wz_b, w4, o
             nc.sync.dma_start(out=dv, in_=sv)
 
         load_rows(x_sb, x, 0, 512)
-        load_w(0, 0)
+        load_w(0, 1)
         load_rows(s0_sb, s0, 0, 1024, 0, 2)
         load_rows(s0_sb, s0, 0, 1024, 2, 4)
-        load_w(0, 1)
-        load_w(1, 0)
-        load_h1(0, 0)
+        load_w(0, 0)
         load_w(1, 1)
+        load_h1(0, 0)
+        load_w(1, 0)
         load_rows(x_sb, x, 1, 512)
         load_rows(s0_sb, s0, 1, 1024)
+        load_w(2, 1)
         load_h1(1, 0)
         load_w(2, 0)
-        load_w(2, 1)
 
         def new_bank(nm):
             return psum.tile([P, 512], F32, name=nm, tag="bank")
@@ -190,11 +190,11 @@ def tile_idrm_ann_pb_kernel(tc, x, s0, h1, ug, wg_w, wg_b, uz, wz_w, wz_b, w4, o
             if G % 2 == 0 and e == 0:
                 if gate == 0:
                     GT[(g, c, n0)] = work.tile(
-                        [P, 4 * N], F32, name="GT%d%d%d" % (g, c, n0), tag=("GT" if N == 512 else "xraw")
+                        [P, 4 * N], F32, name="GT%d%d%d" % (g, c, n0), tag=("GT" if N == 512 or c == 1 else "xraw")
                     )
                 else:
                     ZT[(g, c, n0)] = work.tile(
-                        [P, 4 * N], F32, name="ZT%d%d%d" % (g, c, n0), tag=("ZT" if N == 512 else "s0raw")
+                        [P, 4 * N], F32, name="ZT%d%d%d" % (g, c, n0), tag=("ZT" if N == 512 or c == 1 else "s0raw")
                     )
             acc = new_bank("acc%d%d%d%d%d" % (G, gate, e, c, n0))
             wc = w_c[(G, gate)]
@@ -231,6 +231,20 @@ def tile_idrm_ann_pb_kernel(tc, x, s0, h1, ug, wg_w, wg_b, uz, wz_w, wz_b, w4, o
             d = ZT[(g, c, n0)][:, 2 * u * N : (2 * u + 2) * N].rearrange("p (t n) -> p t n", t=2)
             sv = s0G[c][:].rearrange("p (g n t) -> p g t n", g=2, t=4)[:, g, 2 * u : 2 * u + 2, n0 : n0 + N]
             nc.vector.tensor_tensor(out=d, in0=d, in1=sv, op=ALU.mult)
+
+        def p2one(eng, G, e, c):
+            g = G // 2
+            t = 2 * (G % 2) + e
+            d = ZT[(g, c, 0)][:, t * 512 : (t + 1) * 512]
+            sv = s0G[c][:].rearrange("p (g n t) -> p g t n", g=2, t=4)[:, g, t, :]
+            eng.tensor_tensor(out=d, in0=d, in1=sv, op=ALU.mult)
+
+        def p2half(eng, G, c, n0):
+            g = G // 2
+            u = G % 2
+            d = ZT[(g, c, n0)][:, 2 * u * 256 : (2 * u + 2) * 256].rearrange("p (t n) -> p t n", t=2)
+            sv = s0G[c][:].rearrange("p (g n t) -> p g t n", g=2, t=4)[:, g, 2 * u : 2 * u + 2, n0 : n0 + 256]
+            eng.tensor_tensor(out=d, in0=d, in1=sv, op=ALU.mult)
 
         s1G = {}
 
@@ -320,14 +334,14 @@ def tile_idrm_ann_pb_kernel(tc, x, s0, h1, ug, wg_w, wg_b, uz, wz_w, wz_b, w4, o
 
         prep_x(0, 0)
         prep_x(0, 1)
-        prep_w(0, 0, 0, "V")
+        prep_w(0, 1, 0, "V")
         add_x(0, 0)
-        prep_w(0, 0, 1, "V")
-        prep_w(0, 0, 2, "V")
+        prep_w(0, 1, 1, "V")
+        prep_w(0, 1, 2, "V")
         add_x(0, 1)
         bbank = new_bank("bbank")
         nc.tensor.transpose(bbank[:, 0:P], braw[:], ident[:])
-        quant_w(0, 0)
+        quant_w(0, 1)
         prep_s0(0, 0, 0, "S")
         prep_s0(0, 1, 0, "S")
         quant(x_c[0], x_s[0], xG[0], 0, 512)
@@ -338,12 +352,12 @@ def tile_idrm_ann_pb_kernel(tc, x, s0, h1, ug, wg_w, wg_b, uz, wz_w, wz_b, w4, o
         qs0h(0, 1, 0)
         qs0h(0, 0, 1)
         qs0h(0, 1, 1)
-        prep_w(0, 1, 0, "S")
-        prep_w(0, 1, 1, "S")
-        prep_w(0, 1, 2, "V")
-        quant_w(0, 1)
-        load_w(3, 0)
+        prep_w(0, 0, 0, "S")
+        prep_w(0, 0, 1, "S")
+        prep_w(0, 0, 2, "V")
+        quant_w(0, 0)
         load_w(3, 1)
+        load_w(3, 0)
         load_h1(0, 1)
         load_h1(1, 1)
         nc.sync.dma_start(out=w4_sb[:].rearrange("j (r k) -> j r k", r=2), in_=w4.rearrange("(r j) k -> j r k", j=P))
@@ -366,21 +380,15 @@ def tile_idrm_ann_pb_kernel(tc, x, s0, h1, ug, wg_w, wg_b, uz, wz_w, wz_b, w4, o
 
         hold = {}
 
-        def qw(G, gate, part):
-            if part == 0:
-                quant(w_c[(G, gate)], w_s[(G, gate)], wG[(G, gate)], 0, 512)
-            else:
-                quant(w_c[(G, gate)], w_s[(G, gate)], wG[(G, gate)], 512, 768)
-
         def qs0(c, g):
             quant(s0_c[c], s0_s[c], s0G[c], g * 512, (g + 1) * 512)
 
         def slot(r):
             if r == 0:
                 prep_h1(0, 0)
-                w3(1, 0, "SVS")
-            elif r == 1:
                 w3(1, 1, "SVS")
+            elif r == 1:
+                w3(1, 0, "SVS")
                 prep_x(1, 0)
                 prep_x(1, 1)
             elif r == 2:
@@ -390,31 +398,25 @@ def tile_idrm_ann_pb_kernel(tc, x, s0, h1, ug, wg_w, wg_b, uz, wz_w, wz_b, w4, o
                 prep_s0(1, 1, 0, "V")
                 prep_s0(1, 1, 1, "S")
             elif r == 3:
+                w3(2, 1, "SSS")
+            elif r == 4:
                 prep_h1(0, 1)
-                w3(2, 0)
+                w3(2, 0, "SSS")
             elif r == 5:
+                w3(3, 1, "SSS")
+            elif r == 6:
                 prep_h1(1, 1)
-                w3(2, 1)
-                prep_w(3, 0, 0, "S")
+                w3(3, 0, "SSS")
             elif r == 7:
                 prep_h1(2, 0)
-                prep_w(3, 0, 1, "S")
-                prep_w(3, 0, 2, "S")
-                prep_w(3, 1, 0, "S")
-                prep_w(3, 1, 1, "S")
-            elif r == 9:
                 prep_h1(3, 0)
-                prep_w(3, 1, 2, "S")
-            elif r == 11:
-                prep_h1(2, 1)
-                prep_h1(3, 1)
                 hold["w4G"] = prep_w4()
 
         def vitems(r):
             if r == 0:
-                quant_w(1, 0)
-            elif r == 1:
                 quant_w(1, 1)
+            elif r == 1:
+                quant_w(1, 0)
                 add_x(1, 0)
                 add_x(1, 1)
             elif r == 2:
@@ -422,53 +424,68 @@ def tile_idrm_ann_pb_kernel(tc, x, s0, h1, ug, wg_w, wg_b, uz, wz_w, wz_b, w4, o
                 qs0(1, 0)
                 qs0(1, 1)
             elif r == 3:
+                quant_w(2, 1)
+            elif r == 4:
                 quant_w(2, 0)
             elif r == 5:
-                quant_w(2, 1)
-            elif r == 7:
+                quant_w(3, 1)
+            elif r == 6:
                 quant_w(3, 0)
-                qw(3, 1, 0)
-            elif r == 9:
-                qw(3, 1, 1)
-            elif r == 11:
+            elif r == 7:
                 quant(w4_c, w4_s, hold["w4G"], 0, 512)
 
-        order = ((0, 0), (1, 0), (0, 1), (1, 1), (2, 0), (3, 0))
+        order = ((0, 0), (1, 0), (0, 1), (1, 1))
         for pi, (G, c) in enumerate(order):
-            for gate in range(2):
-                r = 2 * pi + gate
+            for step in range(2):
+                gate = 1 - step
+                r = 2 * pi + step
                 mx_group(G, gate, 0, c)
                 mx_group(G, gate, 1, c)
                 slot(r)
-                if r == 9:
+                if gate == 1:
+                    p2one(nc.vector, G, 0, c)
+                    fill()
                     vitems(r)
-                if gate == 0:
-                    p1(G, c)
+                    fill()
                 else:
-                    p2(G, c)
-                fill()
-                if r != 9:
+                    p2one(nc.gpsimd, G, 1, c)
+                    p1(G, c)
+                    if G % 2 == 1:
+                        queue_add(G // 2, c)
+                    fill()
                     vitems(r)
-                if gate == 1 and G % 2 == 1:
-                    queue_add(G // 2, c)
-                fill()
+                    fill()
 
-        g, c = 1, 1
-        for hh in range(2):
-            n0 = hh * 256
-            for G in (2, 3):
-                for gate in range(2):
-                    for e in range(2):
-                        mx_group(G, gate, e, 1, n0, 256)
-                p1(G, 1, n0, 256)
-                fill(1)
-                p2(G, 1, n0, 256)
-                fill(1)
-            fill(8)
-            add_piece(g, c, 2 * hh, n0)
-            add_piece(g, c, 2 * hh + 1, n0)
-            quant(s1_c[(c, g)], s1_s[(c, g)], s1G[(g, c)], 2 * hh * P, (2 * hh + 1) * P)
-            quant(s1_c[(c, g)], s1_s[(c, g)], s1G[(g, c)], (2 * hh + 1) * P, (2 * hh + 2) * P)
+        g = 1
+        for c in range(2):
+            for hh in range(2):
+                n0 = hh * 256
+                for gate in (1, 0):
+                    for G in (2, 3):
+                        for e in range(2):
+                            mx_group(G, gate, e, c, n0, 256)
+                    if gate == 1:
+                        p2half(nc.vector, 2, c, n0)
+                        fill(1)
+                if c == 0 and hh == 1:
+                    prep_h1(2, 1)
+                    prep_h1(3, 1)
+                p2half(nc.gpsimd, 3, c, n0)
+                p1(2, c, n0, 256)
+                p1(3, c, n0, 256)
+                fill(8)
+                if c == 1 and hh == 1:
+                    add_piece(g, c, 2, n0)
+                    add_piece(g, c, 3, n0)
+                    quant(s1_c[(c, g)], s1_s[(c, g)], s1G[(g, c)], 2 * P, 3 * P)
+                    quant(s1_c[(c, g)], s1_s[(c, g)], s1G[(g, c)], 3 * P, 4 * P)
+                else:
+                    fillers.append(lambda c=c, hh=hh, n0=n0: add_piece(1, c, 2 * hh, n0))
+                    fillers.append(lambda c=c, hh=hh, n0=n0: add_piece(1, c, 2 * hh + 1, n0))
+                    fillers.append(
+                        lambda c=c, hh=hh: quant(s1_c[(c, 1)], s1_s[(c, 1)], s1G[(1, c)], 2 * hh * P, (2 * hh + 2) * P)
+                    )
+                    fill(1)
         stage2(0, 0, "S")
         stage2(0, 1, "S")
         store(0, 1024)

@@ -448,7 +448,7 @@ def tile_idrm_ann_pb_kernel(tc, x, s0, h1, ug, wg_w, wg_b, uz, wz_w, wz_b, w4, o
                     vitems(r)
                     fill()
                 else:
-                    p2one(nc.gpsimd, G, 1, c)
+                    p2one(nc.vector, G, 1, c)
                     p1(G, c)
                     if G % 2 == 1:
                         queue_add(G // 2, c)
@@ -470,7 +470,7 @@ def tile_idrm_ann_pb_kernel(tc, x, s0, h1, ug, wg_w, wg_b, uz, wz_w, wz_b, w4, o
                 if c == 0 and hh == 1:
                     prep_h1(2, 1)
                     prep_h1(3, 1)
-                p2half(nc.gpsimd, 3, c, n0)
+                p2half(nc.vector, 3, c, n0)
                 p1(2, c, n0, 256)
                 p1(3, c, n0, 256)
                 fill(8)

from contextlib import ExitStack

import concourse.mybir as mybir
from concourse.masks import make_identity

FLOPS = 2 * 1024 * 1024 * 1536 * 2 + 2 * 1024 * 1024 * 256

F32 = mybir.dt.float32
BF16 = mybir.dt.bfloat16
U32 = mybir.dt.uint32
U8 = mybir.dt.uint8
FP8X4 = mybir.dt.float8_e4m3fn_x4
ACT = mybir.ActivationFunctionType
ALU = mybir.AluOpType
P = 128


def tile_idrm_ann_pb_kernel(tc, x, s0, h1, ug, wg_w, wg_b, uz, wz_w, wz_b, w4, out):
    nc = tc.nc
    with ExitStack() as ctx:
        keep = ctx.enter_context(tc.tile_pool(name="keep", bufs=1))
        raww = ctx.enter_context(tc.tile_pool(name="raww", bufs=3))
        grp = ctx.enter_context(tc.tile_pool(name="grp", bufs=3))
        work = ctx.enter_context(tc.tile_pool(name="work", bufs=2))
        psum = ctx.enter_context(tc.psum_pool(name="psum", bufs=8))
        ctx.enter_context(tc.manual_schedule())

        ident = keep.tile([P, P], F32, name="ident")
        make_identity(nc, ident[:])
        braw = keep.tile([P, P], F32, name="braw")
        nc.vector.memset(braw[:], 0.0)
        bias = keep.tile([P, 16], F32, name="bias")

        x_sb = [work.tile([P, 4 * 512], BF16, name="x_sb%d" % c, tag="xraw") for c in range(2)]
        s0_sb = [work.tile([P, 4 * 1024], BF16, name="s0_sb%d" % c, tag="s0raw") for c in range(2)]
        h1_sb = {}
        for c in range(2):
            for g in range(2):
                h1_sb[(c, g)] = keep.tile([P, 4 * 512], BF16, name="h1_sb%d%d" % (c, g))
        w4_sb = keep.tile([P, 2 * 1024], BF16, name="w4_sb")
        out_sb = keep.tile([P, 8 * 256], F32, name="out_sb")

        s0G = [keep.tile([P, 4096], BF16, name="s0G%d" % c, align_bytes=64) for c in range(2)]
        x_c = [keep.tile([P, 512], U32, name="x_c%d" % c, align_bytes=64) for c in range(2)]
        x_s = [keep.tile([P, 512], U8, name="x_s%d" % c, align_bytes=64) for c in range(2)]
        s0_c = [keep.tile([P, 1024], U32, name="s0_c%d" % c, align_bytes=64) for c in range(2)]
        s0_s = [keep.tile([P, 1024], U8, name="s0_s%d" % c, align_bytes=64) for c in range(2)]
        w_c = {}
        w_s = {}
        for G in range(4):
            for gate in range(2):
                w_c[(G, gate)] = keep.tile([P, 768], U32, name="w_c%d%d" % (G, gate), align_bytes=64)
                w_s[(G, gate)] = keep.tile([P, 768], U8, name="w_s%d%d" % (G, gate), align_bytes=64)
        w4_c = keep.tile([P, 512], U32, name="w4_c", align_bytes=64)
        w4_s = keep.tile([P, 512], U8, name="w4_s", align_bytes=64)
        s1_c = {}
        s1_s = {}
        for c in range(2):
            for g in range(2):
                s1_c[(c, g)] = keep.tile([P, 512], U32, name="s1_c%d%d" % (c, g), align_bytes=64)
                s1_s[(c, g)] = keep.tile([P, 512], U8, name="s1_s%d%d" % (c, g), align_bytes=64)

        def load_rows(dst, src, c, width, r0=0, r1=4):
            nc.sync.dma_start(
                out=dst[c][:, r0 * width : r1 * width],
                in_=src.rearrange("(p r) k -> p (r k)", r=8)[:, (4 * c + r0) * width : (4 * c + r1) * width],
            )

        raw = {}

        def load_w(G, gate):
            for nm, src, width in ((("ug", ug, 512), ("wg", wg_w, 1024)), (("uz", uz, 512), ("wz", wz_w, 1024)))[gate]:
                t = raww.tile([P, 2 * width], BF16, name="raw_%s%d" % (nm, G), tag="raw_" + nm)
                nc.sync.dma_start(
                    out=t[:], in_=src[256 * G : 256 * G + 256, :].rearrange("(j e) k -> j (e k)", e=2)
                )
                raw[(nm, G)] = t

        bview = braw[:].bitcast(BF16)
        nc.scalar.dma_start(out=bview[0:4, :], in_=wg_b.rearrange("(a w) -> a w", a=4))
        nc.scalar.dma_start(out=bview[4:8, :], in_=wz_b.rearrange("(a w) -> a w", a=4))
        def load_h1(c, g):
            dv = h1_sb[(c, g)][:].rearrange("p (r k) -> p r k", r=4)
            sv = h1.rearrange("(p r) k -> p r k", r=8)[:, 4 * c : 4 * c + 4, g * 512 : (g + 1) * 512]
            nc.sync.dma_start(out=dv, in_=sv)

        load_rows(x_sb, x, 0, 512)
        load_w(0, 1)
        load_rows(s0_sb, s0, 0, 1024, 0, 2)
        load_rows(s0_sb, s0, 0, 1024, 2, 4)
        load_w(0, 0)
        load_w(1, 1)
        load_h1(0, 0)
        load_w(1, 0)
        load_rows(x_sb, x, 1, 512)
        load_rows(s0_sb, s0, 1, 1024)
        load_w(2, 1)
        load_h1(1, 0)
        load_w(2, 0)

        def new_bank(nm):
            return psum.tile([P, 512], F32, name=nm, tag="bank")

        def transposes(nm, srcs):
            bank = new_bank(nm)
            for i, src in enumerate(srcs):
                nc.tensor.transpose(bank[:, i * P : (i + 1) * P], src, ident[:])
            return bank

        def evac_words(eng, dst_words, bank):
            o = dst_words.rearrange("p (n u) -> p n u", u=2)
            i = bank[:].rearrange("p (u n) -> p n u", u=2)
            if eng == "S":
                nc.scalar.copy(out=o, in_=i)
            else:
                nc.vector.tensor_copy(out=o, in_=i)

        def quant(codes, scales, src, a, b):
            nc.vector.quantize_mx(out=codes[:, a:b].bitcast(FP8X4), scales=scales[:, a:b], in_=src[:, 4 * a : 4 * b])

        w4w = w4_sb[:].bitcast(F32)
        xG = {}

        def prep_x(c, h):
            if h == 0:
                xG[c] = grp.tile([P, 2048], BF16, name="xG%d" % c, tag="wG", align_bytes=64)
            srcs = []
            for u in range(2):
                for rr in range(2):
                    o = (2 * h + rr) * 256 + u * P
                    srcs.append(x_sb[c][:].bitcast(F32)[:, o : o + P])
            bank = transposes("tx%d%d" % (c, h), srcs)
            dst = xG[c][:, h * 1024 : (h + 1) * 1024]
            nc.scalar.activation(
                out=dst.rearrange("p (n u e) -> p n u e", u=2, e=2),
                in_=bank[:].bitcast(BF16).rearrange("p (u n e) -> p n u e", u=2, e=2),
                func=ACT.Abs,
            )

        def add_x(c, h):
            dst = xG[c][:, h * 1024 : (h + 1) * 1024]
            nc.vector.tensor_scalar_add(out=dst, in0=dst, scalar1=0.1)

        def prep_s0(c, g, h, eng):
            srcs = []
            for u in range(2):
                for rr in range(2):
                    o = (2 * h + rr) * 512 + g * 256 + u * P
                    srcs.append(s0_sb[c][:].bitcast(F32)[:, o : o + P])
            bank = transposes("ts%d%d%d" % (c, g, h), srcs)
            o = (g * 512 + h * 256) * 2
            evac_words(eng, s0G[c][:].bitcast(F32)[:, o : o + 512], bank)

        wG = {}

        def prep_w(G, gate, k, eng):
            if k == 0:
                wG[(G, gate)] = grp.tile([P, 3072], BF16, name="wG%d%d" % (G, gate), tag="wG", align_bytes=64)
            srcs = []
            for u in range(2):
                for e in range(2):
                    if k == 0:
                        t = raw[(("ug", "uz")[gate], G)]
                        o = e * 256 + u * P
                    else:
                        t = raw[(("wg", "wz")[gate], G)]
                        o = e * 512 + (k - 1) * 256 + u * P
                    srcs.append(t[:].bitcast(F32)[:, o : o + P])
            bank = transposes("tw%d%d%d" % (G, gate, k), srcs)
            evac_words(eng, wG[(G, gate)][:].bitcast(F32)[:, k * 512 : (k + 1) * 512], bank)

        def quant_w(G, gate):
            quant(w_c[(G, gate)], w_s[(G, gate)], wG[(G, gate)], 0, 512)
            quant(w_c[(G, gate)], w_s[(G, gate)], wG[(G, gate)], 512, 768)

        hp = {}

        def prep_h1(G, c):
            srcs = []
            for rr in range(4):
                o = rr * 256 + (G % 2) * P
                srcs.append(h1_sb[(c, G // 2)][:].bitcast(F32)[:, o : o + P])
            hp[(G, c)] = transposes("th%d%d" % (G, c), srcs)

        GT = {}
        ZT = {}

        def mx_group(G, gate, e, c, n0=0, N=512):
            g = G // 2
            if G % 2 == 0 and e == 0:
                if gate == 0:
                    GT[(g, c, n0)] = work.tile(
                        [P, 4 * N], F32, name="GT%d%d%d" % (g, c, n0), tag=("GT" if N == 512 or c == 1 else "xraw")
                    )
                else:
                    ZT[(g, c, n0)] = work.tile(
                        [P, 4 * N], F32, name="ZT%d%d%d" % (g, c, n0), tag=("ZT" if N == 512 or c == 1 else "s0raw")
                    )
            acc = new_bank("acc%d%d%d%d%d" % (G, gate, e, c, n0))
            wc = w_c[(G, gate)]
            ws = w_s[(G, gate)]
            for k in range(3):
                if k == 0:
                    rc, rs, o = x_c[c], x_s[c], n0
                else:
                    rc, rs, o = s0_c[c], s0_s[c], (k - 1) * 512 + n0
                a = k * 256 + e * P
                nc.tensor.matmul_mx(
                    out=acc[:, 0:N],
                    lhsT=wc[:, a : a + P].bitcast(FP8X4),
                    lhsT_scale=ws[:, a : a + P],
                    rhs=rc[:, o : o + N].bitcast(FP8X4),
                    rhs_scale=rs[:, o : o + N],
                    start=(k == 0),
                    stop=(k == 2),
                )
            t = 2 * (G % 2) + e
            dst = (GT, ZT)[gate][(g, c, n0)][:, t * N : (t + 1) * N]
            col = (gate * 4 + G) * 2 + e
            nc.scalar.activation(out=dst, in_=acc[:, 0:N], func=ACT.Tanh, bias=bias[:, col : col + 1], scale=1.0)

        def p1(G, c, n0=0, N=512):
            u = G % 2
            d = GT[(G // 2, c, n0)][:, 2 * u * N : (2 * u + 2) * N].rearrange("p (t n) -> p t n", t=2)
            hv = hp[(G, c)][:].bitcast(BF16).rearrange("p (n e) -> p e n", e=2)[:, :, n0 : n0 + N]
            nc.vector.scalar_tensor_tensor(out=d, in0=d, scalar=-1.0, in1=hv, op0=ALU.add, op1=ALU.mult)

        def p2(G, c, n0=0, N=512):
            g = G // 2
            u = G % 2
            d = ZT[(g, c, n0)][:, 2 * u * N : (2 * u + 2) * N].rearrange("p (t n) -> p t n", t=2)
            sv = s0G[c][:].rearrange("p (g n t) -> p g t n", g=2, t=4)[:, g, 2 * u : 2 * u + 2, n0 : n0 + N]
            nc.vector.tensor_tensor(out=d, in0=d, in1=sv, op=ALU.mult)

        def p2one(eng, G, e, c):
            g = G // 2
            t = 2 * (G % 2) + e
            d = ZT[(g, c, 0)][:, t * 512 : (t + 1) * 512]
            sv = s0G[c][:].rearrange("p (g n t) -> p g t n", g=2, t=4)[:, g, t, :]
            eng.tensor_tensor(out=d, in0=d, in1=sv, op=ALU.mult)

        def p2half(eng, G, c, n0):
            g = G // 2
            u = G % 2
            d = ZT[(g, c, n0)][:, 2 * u * 256 : (2 * u + 2) * 256].rearrange("p (t n) -> p t n", t=2)
            sv = s0G[c][:].rearrange("p (g n t) -> p g t n", g=2, t=4)[:, g, 2 * u : 2 * u + 2, n0 : n0 + 256]
            eng.tensor_tensor(out=d, in0=d, in1=sv, op=ALU.mult)

        s1G = {}

        def add_piece(g, c, q, n0=0):
            if q == 0:
                s1G[(g, c)] = work.tile([P, 2048], BF16, name="s1G%d%d" % (g, c), tag="s1G", align_bytes=64)
            m0 = q * P
            o = s1G[(g, c)][:, 4 * m0 : 4 * (m0 + P)].rearrange("p (c i t) -> p c t i", i=4, t=4)
            lo = m0 - n0
            a = ZT[(g, c, n0)][:].rearrange("p (t n) -> p t n", t=4)[:, :, lo : lo + P].rearrange("p t (c i) -> p c t i", i=4)
            b = GT[(g, c, n0)][:].rearrange("p (t n) -> p t n", t=4)[:, :, lo : lo + P].rearrange("p t (c i) -> p c t i", i=4)
            nc.vector.tensor_tensor(out=o, in0=a, in1=b, op=ALU.subtract)

        def stage2(c, h, eng):
            bank = new_bank("o%d%d" % (c, h))
            for rr in range(2):
                a = (2 * h + rr) * P
                for g in range(2):
                    nc.tensor.matmul_mx(
                        out=bank[:, rr * 256 : (rr + 1) * 256],
                        lhsT=s1_c[(c, g)][:, a : a + P].bitcast(FP8X4),
                        lhsT_scale=s1_s[(c, g)][:, a : a + P],
                        rhs=w4_c[:, g * 256 : (g + 1) * 256].bitcast(FP8X4),
                        rhs_scale=w4_s[:, g * 256 : (g + 1) * 256],
                        start=(g == 0),
                        stop=(g == 1),
                    )
            o = (4 * c + 2 * h) * 256
            if eng == "S":
                nc.scalar.copy(out=out_sb[:, o : o + 512], in_=bank[:])
            else:
                nc.vector.tensor_copy(out=out_sb[:, o : o + 512], in_=bank[:])

        obank = {}

        def stage2_open(c, rr):
            obank[(c, rr)] = new_bank("oo%d%d" % (c, rr))
            a = rr * P
            nc.tensor.matmul_mx(
                out=obank[(c, rr)][:, 0:256],
                lhsT=s1_c[(c, 0)][:, a : a + P].bitcast(FP8X4),
                lhsT_scale=s1_s[(c, 0)][:, a : a + P],
                rhs=w4_c[:, 0:256].bitcast(FP8X4),
                rhs_scale=w4_s[:, 0:256],
                start=True,
                stop=False,
            )

        def stage2_close(c, rr, eng):
            a = rr * P
            nc.tensor.matmul_mx(
                out=obank[(c, rr)][:, 0:256],
                lhsT=s1_c[(c, 1)][:, a : a + P].bitcast(FP8X4),
                lhsT_scale=s1_s[(c, 1)][:, a : a + P],
                rhs=w4_c[:, 256:512].bitcast(FP8X4),
                rhs_scale=w4_s[:, 256:512],
                start=False,
                stop=True,
            )
            o = (4 * c + rr) * 256
            if eng == "S":
                nc.scalar.copy(out=out_sb[:, o : o + 256], in_=obank[(c, rr)][:, 0:256])
            else:
                nc.vector.tensor_copy(out=out_sb[:, o : o + 256], in_=obank[(c, rr)][:, 0:256])

        out_v = out.rearrange("(p r) n -> p (r n)", r=8)

        def store(a, b):
            nc.sync.dma_start(out=out_v[:, a:b], in_=out_sb[:, a:b])

        fillers = []
        done = [0]

        def fill(n=1):
            for i in range(n):
                if done[0] < len(fillers):
                    fillers[done[0]]()
                    done[0] += 1

        def queue_add(g, c):
            for q in range(4):
                fillers.append(lambda q=q: add_piece(g, c, q))
            fillers.append(lambda: quant(s1_c[(c, g)], s1_s[(c, g)], s1G[(g, c)], 0, 512))

        def qs0h(c, g, h):
            quant(s0_c[c], s0_s[c], s0G[c], g * 512 + h * 256, g * 512 + (h + 1) * 256)

        prep_x(0, 0)
        prep_x(0, 1)
        prep_w(0, 1, 0, "V")
        add_x(0, 0)
        prep_w(0, 1, 1, "V")
        prep_w(0, 1, 2, "V")
        add_x(0, 1)
        bbank = new_bank("bbank")
        nc.tensor.transpose(bbank[:, 0:P], braw[:], ident[:])
        quant_w(0, 1)
        prep_s0(0, 0, 0, "S")
        prep_s0(0, 1, 0, "S")
        quant(x_c[0], x_s[0], xG[0], 0, 512)
        nc.vector.tensor_copy(out=bias[:], in_=bbank[:].bitcast(BF16)[:, 0:16])
        qs0h(0, 0, 0)
        prep_s0(0, 0, 1, "S")
        prep_s0(0, 1, 1, "V")
        qs0h(0, 1, 0)
        qs0h(0, 0, 1)
        qs0h(0, 1, 1)
        prep_w(0, 0, 0, "S")
        prep_w(0, 0, 1, "S")
        prep_w(0, 0, 2, "V")
        quant_w(0, 0)
        load_w(3, 1)
        load_w(3, 0)
        load_h1(0, 1)
        load_h1(1, 1)
        nc.sync.dma_start(out=w4_sb[:].rearrange("j (r k) -> j r k", r=2), in_=w4.rearrange("(r j) k -> j r k", j=P))

        def prep_w4():
            w4G = grp.tile([P, 2048], BF16, name="w4G", tag="wG", align_bytes=64)
            for g in range(2):
                srcs = []
                for u in range(2):
                    for ro in range(2):
                        o = ro * 512 + g * 256 + u * P
                        srcs.append(w4w[:, o : o + P])
                bank = transposes("t4%d" % g, srcs)
                evac_words("S", w4G[:].bitcast(F32)[:, g * 512 : (g + 1) * 512], bank)
            return w4G

        def w3(G, gate, engs="SSS"):
            for k in range(3):
                prep_w(G, gate, k, engs[k])

        hold = {}

        def qs0(c, g):
            quant(s0_c[c], s0_s[c], s0G[c], g * 512, (g + 1) * 512)

        def slot(r):
            if r == 0:
                prep_h1(0, 0)
                w3(1, 1, "SVS")
            elif r == 1:
                w3(1, 0, "SVS")
                prep_x(1, 0)
                prep_x(1, 1)
            elif r == 2:
                prep_h1(1, 0)
                prep_s0(1, 0, 0, "S")
                prep_s0(1, 0, 1, "S")
                prep_s0(1, 1, 0, "V")
                prep_s0(1, 1, 1, "S")
            elif r == 3:
                w3(2, 1, "SSS")
            elif r == 4:
                prep_h1(0, 1)
                w3(2, 0, "SSS")
            elif r == 5:
                w3(3, 1, "SSS")
            elif r == 6:
                prep_h1(1, 1)
                w3(3, 0, "SSS")
            elif r == 7:
                prep_h1(2, 0)
                prep_h1(3, 0)
                hold["w4G"] = prep_w4()

        def vitems(r):
            if r == 0:
                quant_w(1, 1)
            elif r == 1:
                quant_w(1, 0)
                add_x(1, 0)
                add_x(1, 1)
            elif r == 2:
                quant(x_c[1], x_s[1], xG[1], 0, 512)
                qs0(1, 0)
                qs0(1, 1)
            elif r == 3:
                quant_w(2, 1)
            elif r == 4:
                quant_w(2, 0)
            elif r == 5:
                quant_w(3, 1)
            elif r == 6:
                quant_w(3, 0)
            elif r == 7:
                quant(w4_c, w4_s, hold["w4G"], 0, 512)

        order = ((0, 0), (1, 0), (0, 1), (1, 1))
        for pi, (G, c) in enumerate(order):
            for step in range(2):
                gate = 1 - step
                r = 2 * pi + step
                mx_group(G, gate, 0, c)
                mx_group(G, gate, 1, c)
                slot(r)
                if gate == 1:
                    p2one(nc.vector, G, 0, c)
                    fill()
                    vitems(r)
                    fill()
                else:
                    p2one(nc.vector, G, 1, c)
                    p1(G, c)
                    if G % 2 == 1:
                        queue_add(G // 2, c)
                    fill()
                    vitems(r)
                    fill()

        g = 1
        for c in range(2):
            for hh in range(2):
                n0 = hh * 256
                for gate in (1, 0):
                    for G in (2, 3):
                        for e in range(2):
                            mx_group(G, gate, e, c, n0, 256)
                    if gate == 1:
                        p2half(nc.vector, 2, c, n0)
                        fill(1)
                if c == 0 and hh == 1:
                    prep_h1(2, 1)
                    prep_h1(3, 1)
                p2half(nc.vector, 3, c, n0)
                p1(2, c, n0, 256)
                p1(3, c, n0, 256)
                fill(8)
                if c == 1 and hh == 1:
                    add_piece(g, c, 2, n0)
                    add_piece(g, c, 3, n0)
                    quant(s1_c[(c, g)], s1_s[(c, g)], s1G[(g, c)], 2 * P, 3 * P)
                    quant(s1_c[(c, g)], s1_s[(c, g)], s1G[(g, c)], 3 * P, 4 * P)
                else:
                    fillers.append(lambda c=c, hh=hh, n0=n0: add_piece(1, c, 2 * hh, n0))
                    fillers.append(lambda c=c, hh=hh, n0=n0: add_piece(1, c, 2 * hh + 1, n0))
                    fillers.append(
                        lambda c=c, hh=hh: quant(s1_c[(c, 1)], s1_s[(c, 1)], s1G[(1, c)], 2 * hh * P, (2 * hh + 2) * P)
                    )
                    fill(1)
        stage2(0, 0, "S")
        stage2(0, 1, "S")
        store(0, 1024)
        for rr in range(4):
            stage2_open(1, rr)
        stage2_close(1, 0, "S")
        stage2_close(1, 1, "S")
        store(1024, 1536)
        stage2_close(1, 2, "S")
        store(1536, 1792)
        stage2_close(1, 3, "V")
        store(1792, 2048)
